import numpy as np
import ml_dtypes


def mxq(x, axis, fmt="e4m3"):
    dtype, down = {"e4m3": (ml_dtypes.float8_e4m3fn, 7), "e5m2": (ml_dtypes.float8_e5m2, 14)}[fmt]
    v = np.moveaxis(np.asarray(x, np.float32).astype(ml_dtypes.bfloat16).astype(np.float64), axis, -1)
    blocks = v.reshape(v.shape[:-1] + (-1, 32))
    amax = np.abs(blocks).max(-1, keepdims=True)
    byte = np.maximum(np.where(amax > 0, np.frexp(amax)[1] - 1 + 127, 0) - down, 1)
    scale = np.exp2(byte - 127.0)
    codes = (blocks / scale).astype(np.float32).astype(dtype).astype(np.float64)
    return np.moveaxis((codes * scale).reshape(v.shape), -1, axis)


WIDE = False


def mx_kscale(k):
    if not WIDE:
        return np.ones(k)
    levels = np.array([10, -10, 5, -5, 0])
    a = np.random.permutation(np.resize(levels, k // 512 * 4)).reshape(k // 512, 4)
    idx = np.arange(k)
    return np.exp2(a[idx // 512, idx % 128 // 32])


BF16 = ml_dtypes.bfloat16


def bf(x):
    return np.asarray(x, np.float32).astype(BF16)


def f64(x):
    return np.asarray(x).astype(np.float64)


E2M1 = np.array([0.0, 0.5, 1.0, 1.5, 2.0, 3.0, 4.0, 6.0, -0.0, -0.5, -1.0, -1.5, -2.0, -3.0, -4.0, -6.0])


def pack_weight(w, fmt):
    k, n = w.shape
    w = f64(bf(w)).reshape(k // 32, 32, n)
    amax = np.abs(w).max(1)
    if fmt == "e4m3":
        byte = np.frexp(amax)[1] - 1 + 127 - 7
    else:
        mant, ex = np.frexp(amax / 6.0)
        byte = np.where(mant > 0.5, ex, ex - 1) + 127
    byte = np.clip(np.where(amax > 0, byte, 1), 1, 254)
    scaled = (w * np.exp2(127.0 - byte)[:, None, :]).reshape(k, n).astype(np.float32)
    by_word = np.ascontiguousarray(scaled.reshape(k // 512, 128, 4, n).transpose(0, 1, 3, 2))
    if fmt == "e4m3":
        words = by_word.astype(ml_dtypes.float8_e4m3fn).view(np.uint8)
    else:
        c = by_word.astype(ml_dtypes.float4_e2m1fn).view(np.uint8) & 0xF
        words = c[..., 0::2] | (c[..., 1::2] << 4)
    return np.ascontiguousarray(words), np.ascontiguousarray(byte.astype(np.uint8).reshape(k // 512, 16, n))


def unpack_weight(words, scales, fmt):
    g, p, n, _ = words.shape
    if fmt == "e4m3":
        vals = np.ascontiguousarray(words).view(ml_dtypes.float8_e4m3fn).astype(np.float64)
    else:
        nib = np.empty((g, p, n, 4), np.uint8)
        nib[..., 0::2] = words & 0xF
        nib[..., 1::2] = words >> 4
        vals = E2M1[nib]
    vals = vals * np.repeat(np.exp2(scales.astype(np.float64) - 127.0), 8, axis=1)[..., None]
    return vals.transpose(0, 1, 3, 2).reshape(g * 512, n)


N, D, O, H, W = 8, 512, 128, 32, 32
K = D + D
P = H * W


def exp_softmax_pool(y):
    a = np.exp(y)
    e = np.exp(a - a.max(-1, keepdims=True))
    sm = e / e.sum(-1, keepdims=True)
    return (sm * y).sum(-1)


def setup_inputs():
    s = mx_kscale(K)
    x1 = bf(np.random.standard_normal((N, D, H, W)) * 0.5 * s[:D][None, :, None, None])
    x2 = bf(np.random.standard_normal((N, D, H, W)) * 0.5 * s[D:][None, :, None, None])
    c1_w_words, c1_w_scales = pack_weight((np.random.standard_normal((O, K)) / np.sqrt(K) / s).T, "e4m3")
    c1_b = bf(np.random.standard_normal(O) * 0.3)
    c2_w_words, c2_w_scales = pack_weight((np.random.standard_normal((O, K)) / np.sqrt(K) / s).T, "e4m3")
    c2_b = bf(np.random.standard_normal(O) * 0.3)
    return {"x1": x1,
            "x2": x2,
            "c1_w_words": c1_w_words, "c1_w_scales": c1_w_scales, "c1_b": c1_b,
            "c2_w_words": c2_w_words, "c2_w_scales": c2_w_scales, "c2_b": c2_b}


def reference(x1, x2, c1_w_words, c1_w_scales, c1_b, c2_w_words, c2_w_scales, c2_b):
    xc = np.concatenate([f64(x1), f64(x2)], axis=1).reshape(N, K, P)
    xq = mxq(xc, 1, "e4m3")
    x1x = (unpack_weight(c1_w_words, c1_w_scales, "e4m3").T @ xq) + f64(c1_b)[None, :, None]
    x2x = (unpack_weight(c2_w_words, c2_w_scales, "e4m3").T @ xq) + f64(c2_b)[None, :, None]
    return exp_softmax_pool(x1x), exp_softmax_pool(x2x)

@@ -1,0 +1,204 @@
+from contextlib import ExitStack
+
+import concourse.mybir as mybir
+from concourse.masks import make_identity
+
+FP8X4 = mybir.dt.float8_e4m3fn_x4
+BF16 = mybir.dt.bfloat16
+F32 = mybir.dt.float32
+U32 = mybir.dt.uint32
+U8 = mybir.dt.uint8
+EXP = mybir.ActivationFunctionType.Exp
+ALU = mybir.AluOpType
+AXIS_X = mybir.AxisListType.X
+
+P = 128
+PACK = 4
+BATCH = 8
+STREAMS = 2
+POSITIONS = 1024
+HALF = 512
+HALVES = POSITIONS // HALF
+HEADS = 2
+OUT = 128
+RUN = 4
+
+FLOPS = 2 * BATCH * HEADS * OUT * STREAMS * P * PACK * POSITIONS
+
+
+def tile_fr_pa_t_kernel(
+    tc, x1, x2, c1_w_words, c1_w_scales, c1_b, c2_w_words, c2_w_scales, c2_b, out_0, out_1
+):
+    nc = tc.nc
+    streams = (x1, x2)
+    weights = ((c1_w_words, c1_w_scales, c1_b), (c2_w_words, c2_w_scales, c2_b))
+
+    with ExitStack() as ctx:
+        keep = ctx.enter_context(tc.tile_pool(name="keep", bufs=1))
+        group_pool = ctx.enter_context(tc.tile_pool(name="group", bufs=3))
+        code_pool = ctx.enter_context(tc.tile_pool(name="code", bufs=4))
+        soft_pool = ctx.enter_context(tc.tile_pool(name="soft", bufs=3))
+        psum = ctx.enter_context(tc.psum_pool(name="psum", bufs=4))
+        ctx.enter_context(tc.manual_schedule())
+
+        raw_of = {}
+        grouped_of = {}
+        codes_of = {}
+        planes_of = {}
+        y_of = {}
+        a_of = {}
+        e_of = {}
+
+        w_codes = keep.tile([P, HEADS, STREAMS, OUT], U32, align_bytes=64)
+        w_planes = keep.tile([P, HEADS, STREAMS, OUT], U8, align_bytes=64)
+        nc.vector.memset(w_planes[:].rearrange("p i g o -> p (i g o)").bitcast(mybir.dt.int32), 0)
+        bias_of = {}
+        for i, (words, scales, b) in enumerate(weights):
+            bias = keep.tile([P, 1], BF16, name="bias_%d" % i)
+            nc.scalar.dma_start(out=bias[:], in_=b.rearrange("(o one) -> o one", one=1))
+            bias_of[i] = bias
+
+        for n in range(BATCH):
+            for h in range(HALVES):
+                raw = keep.tile([P, STREAMS, PACK, HALF], BF16, name="raw_%d_%d" % (n, h))
+                for g, x in enumerate(streams):
+                    rows = x[n].rearrange("(p j) a b -> p j (a b)", j=PACK)
+                    nc.sync.dma_start(out=raw[:, g], in_=rows[:, :, h * HALF : (h + 1) * HALF])
+                raw_of[(n, h)] = raw
+
+        for i, (words, scales, b) in enumerate(weights):
+            for quadrant in range(4):
+                nc.gpsimd.dma_start(
+                    out=w_planes[32 * quadrant : 32 * quadrant + 4, i].bitcast(F32),
+                    in_=scales[:, 4 * quadrant : 4 * quadrant + 4, :].rearrange("g r o -> r g o").bitcast(F32),
+                )
+            nc.gpsimd.dma_start(
+                out=w_codes[:, i].bitcast(F32),
+                in_=words.rearrange("g p o t -> p g (o t)").bitcast(F32),
+            )
+
+        identity = keep.tile([P, P], F32)
+        make_identity(nc, identity[:])
+        pooled = keep.tile([P, P], F32)
+        nc.gpsimd.memset(pooled[:], 0.0)
+
+        neg_top = keep.tile([P, HEADS, BATCH], F32)
+        weight_sum = keep.tile([P, HEADS, BATCH], F32)
+        value_sum = keep.tile([P, HEADS, BATCH, HALVES], F32)
+
+        def regroup(n, h):
+            raw = raw_of[(n, h)]
+            grouped = group_pool.tile([P, STREAMS, HALF, PACK], BF16, align_bytes=64)
+            nc.vector.tensor_copy(
+                out=grouped[:, 0].rearrange("p (c r) j -> p c j r", r=RUN),
+                in_=raw[:, 0].rearrange("p j (c r) -> p c j r", r=RUN),
+            )
+            nc.scalar.copy(
+                out=grouped[:, 1].rearrange("p (c r) j -> p c j r", r=RUN),
+                in_=raw[:, 1].rearrange("p j (c r) -> p c j r", r=RUN),
+            )
+            grouped_of[(n, h)] = grouped
+
+        def quantise(n, h):
+            codes = code_pool.tile([P, STREAMS, HALF], U32, align_bytes=64)
+            planes = code_pool.tile([P, STREAMS, HALF], U8, align_bytes=64)
+            nc.vector.quantize_mx(
+                out=codes[:].rearrange("p g w -> p (g w)").bitcast(FP8X4),
+                scales=planes[:].rearrange("p g w -> p (g w)"),
+                in_=grouped_of[(n, h)][:].rearrange("p g w j -> p (g w j)"),
+            )
+            codes_of[(n, h)] = codes
+            planes_of[(n, h)] = planes
+
+        def project(n, i):
+            y = psum.tile([P, HALVES, HALF], F32)
+            for h in range(HALVES):
+                for g in range(STREAMS):
+                    nc.tensor.matmul_mx(
+                        out=y[:, h, :],
+                        lhsT=w_codes[:, i, g, :].bitcast(FP8X4),
+                        lhsT_scale=w_planes[:, i, g, :],
+                        rhs=codes_of[(n, h)][:, g, :].bitcast(FP8X4),
+                        rhs_scale=planes_of[(n, h)][:, g, :],
+                        start=(g == 0),
+                        stop=(g == STREAMS - 1),
+                    )
+            y_of[(n, i)] = y
+
+        def first_exp(n, i):
+            a = soft_pool.tile([P, HALVES, HALF], F32)
+            for h in range(HALVES):
+                nc.scalar.activation(out=a[:, h, :], in_=y_of[(n, i)][:, h, :], func=EXP, bias=bias_of[i][:])
+            a_of[(n, i)] = a
+
+        def top(n, i):
+            nc.vector.tensor_reduce(
+                out=neg_top[:, i, n : n + 1],
+                in_=a_of[(n, i)][:].rearrange("p h w -> p (h w)"),
+                axis=AXIS_X,
+                op=ALU.max,
+                negate=True,
+            )
+
+        def second_exp(n, i):
+            e = soft_pool.tile([P, HALVES, HALF], F32)
+            nc.scalar.activation(
+                out=e[:].rearrange("p h w -> p (h w)"),
+                in_=a_of[(n, i)][:].rearrange("p h w -> p (h w)"),
+                func=EXP,
+                bias=neg_top[:, i, n : n + 1],
+                accum_out=weight_sum[:, i, n : n + 1],
+            )
+            e_of[(n, i)] = e
+
+        def weigh(n, i):
+            e = e_of[(n, i)]
+            for h in range(HALVES):
+                nc.vector.scalar_tensor_tensor(
+                    out=e[:, h, :],
+                    in0=y_of[(n, i)][:, h, :],
+                    scalar=bias_of[i][:],
+                    in1=e[:, h, :],
+                    op0=ALU.add,
+                    op1=ALU.mult,
+                    accum_out=value_sum[:, i, n, h : h + 1],
+                )
+
+        for t in range(BATCH + 2):
+            front = t < BATCH
+            back = t - 2
+            if 1 <= t <= BATCH:
+                quantise(t - 1, 1)
+                for i in range(HEADS):
+                    project(t - 1, i)
+            if back >= 0:
+                for i in range(HEADS):
+                    first_exp(back, i)
+            if front:
+                regroup(t, 0)
+            if back >= 0:
+                for i in range(HEADS):
+                    top(back, i)
+                for i in range(HEADS):
+                    second_exp(back, i)
+            if front:
+                regroup(t, 1)
+                quantise(t, 0)
+            if back >= 0:
+                for i in range(HEADS):
+                    weigh(back, i)
+
+        columns = HEADS * BATCH
+        value_total = keep.tile([P, columns], F32)
+        nc.vector.tensor_reduce(
+            out=value_total[:], in_=value_sum[:].rearrange("p i n h -> p (i n) h"), axis=AXIS_X, op=ALU.add
+        )
+        inverse = keep.tile([P, columns], F32)
+        nc.vector.reciprocal(out=inverse[:], in_=weight_sum[:].rearrange("p i n -> p (i n)"))
+        nc.vector.tensor_tensor(out=pooled[:, 0:columns], in0=value_total[:], in1=inverse[:], op=ALU.mult)
+        flipped = psum.tile([P, HALVES, HALF], F32, tag="y")
+        nc.tensor.transpose(flipped[:, 0, 0:P], pooled[:], identity[:])
+        rows_out = keep.tile([P, P], F32)
+        nc.vector.tensor_copy(out=rows_out[:], in_=flipped[:, 0, 0:P])
+        nc.sync.dma_start(out=out_0, in_=rows_out[0:BATCH, :])
+        nc.sync.dma_start(out=out_1, in_=rows_out[BATCH : 2 * BATCH, :])

@@ -8,6 +8,7 @@ BF16 = mybir.dt.bfloat16
 F32 = mybir.dt.float32
 U32 = mybir.dt.uint32
 U8 = mybir.dt.uint8
+I32 = mybir.dt.int32
 EXP = mybir.ActivationFunctionType.Exp
 ALU = mybir.AluOpType
 AXIS_X = mybir.AxisListType.X
@@ -51,31 +52,47 @@ def tile_fr_pa_t_kernel(
 
         w_codes = keep.tile([P, HEADS, STREAMS, OUT], U32, align_bytes=64)
         w_planes = keep.tile([P, HEADS, STREAMS, OUT], U8, align_bytes=64)
-        nc.vector.memset(w_planes[:].rearrange("p i g o -> p (i g o)").bitcast(mybir.dt.int32), 0)
+        nc.vector.memset(w_planes[:].rearrange("p i g o -> p (i g o)").bitcast(I32), 0)
         bias_of = {}
-        for i, (words, scales, b) in enumerate(weights):
+
+        def load_weight(i):
+            words, scales, b = weights[i]
+            for quadrant in range(4):
+                nc.sync.dma_start(
+                    out=w_planes[32 * quadrant : 32 * quadrant + 4, i].bitcast(I32),
+                    in_=scales[:, 4 * quadrant : 4 * quadrant + 4, :].rearrange("g r o -> r g o").bitcast(I32),
+                )
+            nc.sync.dma_start(
+                out=w_codes[:, i].bitcast(I32),
+                in_=words.rearrange("g p o t -> p g (o t)").bitcast(I32),
+            )
+
+        def load_bias(i):
+            words, scales, b = weights[i]
             bias = keep.tile([P, 1], BF16, name="bias_%d" % i)
-            nc.scalar.dma_start(out=bias[:], in_=b.rearrange("(o one) -> o one", one=1))
+            nc.sync.dma_start(out=bias[:], in_=b.rearrange("(o one) -> o one", one=1))
             bias_of[i] = bias
 
-        for n in range(BATCH):
-            for h in range(HALVES):
-                raw = keep.tile([P, STREAMS, PACK, HALF], BF16, name="raw_%d_%d" % (n, h))
-                for g, x in enumerate(streams):
-                    rows = x[n].rearrange("(p j) a b -> p j (a b)", j=PACK)
-                    nc.sync.dma_start(out=raw[:, g], in_=rows[:, :, h * HALF : (h + 1) * HALF])
-                raw_of[(n, h)] = raw
+        def load_x(n, h):
+            raw = keep.tile([P, STREAMS, PACK, HALF], BF16, name="raw_%d_%d" % (n, h))
+            for g, x in enumerate(streams):
+                rows = x[n].rearrange("(p j) a b -> p j (a b)", j=PACK)
+                nc.sync.dma_start(out=raw[:, g], in_=rows[:, :, h * HALF : (h + 1) * HALF])
+            raw_of[(n, h)] = raw
 
-        for i, (words, scales, b) in enumerate(weights):
-            for quadrant in range(4):
-                nc.gpsimd.dma_start(
-                    out=w_planes[32 * quadrant : 32 * quadrant + 4, i].bitcast(F32),
-                    in_=scales[:, 4 * quadrant : 4 * quadrant + 4, :].rearrange("g r o -> r g o").bitcast(F32),
-                )
-            nc.gpsimd.dma_start(
-                out=w_codes[:, i].bitcast(F32),
-                in_=words.rearrange("g p o t -> p g (o t)").bitcast(F32),
-            )
+        load_weight(0)
+        load_x(0, 0)
+        load_weight(1)
+        load_x(0, 1)
+        load_bias(0)
+        load_bias(1)
+        for n in range(1, BATCH):
+            for h in range(HALVES):
+                load_x(n, h)
+
+        warm = keep.tile([P, 1], F32)
+        nc.vector.memset(warm[:], 0.0)
+        nc.scalar.activation(out=warm[:], in_=warm[:], func=EXP)
 
         identity = keep.tile([P, P], F32)
         make_identity(nc, identity[:])
@@ -86,18 +103,19 @@ def tile_fr_pa_t_kernel(
         weight_sum = keep.tile([P, HEADS, BATCH], F32)
         value_sum = keep.tile([P, HEADS, BATCH, HALVES], F32)
 
-        def regroup(n, h):
-            raw = raw_of[(n, h)]
+        def regroup_x1(n, h):
             grouped = group_pool.tile([P, STREAMS, HALF, PACK], BF16, align_bytes=64)
             nc.vector.tensor_copy(
                 out=grouped[:, 0].rearrange("p (c r) j -> p c j r", r=RUN),
-                in_=raw[:, 0].rearrange("p j (c r) -> p c j r", r=RUN),
-            )
-            nc.scalar.copy(
-                out=grouped[:, 1].rearrange("p (c r) j -> p c j r", r=RUN),
-                in_=raw[:, 1].rearrange("p j (c r) -> p c j r", r=RUN),
+                in_=raw_of[(n, h)][:, 0].rearrange("p j (c r) -> p c j r", r=RUN),
             )
             grouped_of[(n, h)] = grouped
+
+        def regroup_x2(n, h):
+            nc.scalar.copy(
+                out=grouped_of[(n, h)][:, 1].rearrange("p (c r) j -> p c j r", r=RUN),
+                in_=raw_of[(n, h)][:, 1].rearrange("p j (c r) -> p c j r", r=RUN),
+            )
 
         def quantise(n, h):
             codes = code_pool.tile([P, STREAMS, HALF], U32, align_bytes=64)
@@ -167,6 +185,8 @@ def tile_fr_pa_t_kernel(
         for t in range(BATCH + 2):
             front = t < BATCH
             back = t - 2
+            if front:
+                regroup_x1(t, 0)
             if 1 <= t <= BATCH:
                 quantise(t - 1, 1)
                 for i in range(HEADS):
@@ -175,14 +195,15 @@ def tile_fr_pa_t_kernel(
                 for i in range(HEADS):
                     first_exp(back, i)
             if front:
-                regroup(t, 0)
+                regroup_x2(t, 0)
             if back >= 0:
                 for i in range(HEADS):
                     top(back, i)
                 for i in range(HEADS):
                     second_exp(back, i)
             if front:
-                regroup(t, 1)
+                regroup_x1(t, 1)
+                regroup_x2(t, 1)
                 quantise(t, 0)
             if back >= 0:
                 for i in range(HEADS):

@@ -23,6 +23,10 @@ HALVES = POSITIONS // HALF
 HEADS = 2
 OUT = 128
 RUN = 4
+COLUMNS = STREAMS * HALF
+VECTOR_COLUMNS = 320
+GPSIMD_COLUMNS = 256
+SCALAR_COLUMNS = COLUMNS - VECTOR_COLUMNS - GPSIMD_COLUMNS
 
 FLOPS = 2 * BATCH * HEADS * OUT * STREAMS * P * PACK * POSITIONS
 
@@ -36,7 +40,7 @@ def tile_fr_pa_t_kernel(
 
     with ExitStack() as ctx:
         keep = ctx.enter_context(tc.tile_pool(name="keep", bufs=1))
-        group_pool = ctx.enter_context(tc.tile_pool(name="group", bufs=3))
+        group_pool = ctx.enter_context(tc.tile_pool(name="group", bufs=2))
         code_pool = ctx.enter_context(tc.tile_pool(name="code", bufs=4))
         soft_pool = ctx.enter_context(tc.tile_pool(name="soft", bufs=3))
         psum = ctx.enter_context(tc.psum_pool(name="psum", bufs=4))
@@ -74,10 +78,12 @@ def tile_fr_pa_t_kernel(
             bias_of[i] = bias
 
         def load_x(n, h):
-            raw = keep.tile([P, STREAMS, PACK, HALF], BF16, name="raw_%d_%d" % (n, h))
+            raw = keep.tile([P, PACK, COLUMNS], BF16, name="raw_%d_%d" % (n, h))
             for g, x in enumerate(streams):
                 rows = x[n].rearrange("(p j) a b -> p j (a b)", j=PACK)
-                nc.sync.dma_start(out=raw[:, g], in_=rows[:, :, h * HALF : (h + 1) * HALF])
+                nc.sync.dma_start(
+                    out=raw[:, :, g * HALF : (g + 1) * HALF], in_=rows[:, :, h * HALF : (h + 1) * HALF]
+                )
             raw_of[(n, h)] = raw
 
         load_weight(0)
@@ -103,18 +109,31 @@ def tile_fr_pa_t_kernel(
         weight_sum = keep.tile([P, HEADS, BATCH], F32)
         value_sum = keep.tile([P, HEADS, BATCH, HALVES], F32)
 
-        def regroup_x1(n, h):
-            grouped = group_pool.tile([P, STREAMS, HALF, PACK], BF16, align_bytes=64)
+        def regroup_on_vector(n, h):
+            grouped = group_pool.tile([P, COLUMNS, PACK], BF16, align_bytes=64)
+            share = slice(0, VECTOR_COLUMNS)
             nc.vector.tensor_copy(
-                out=grouped[:, 0].rearrange("p (c r) j -> p c j r", r=RUN),
-                in_=raw_of[(n, h)][:, 0].rearrange("p j (c r) -> p c j r", r=RUN),
+                out=grouped[:, share, :].rearrange("p (c r) j -> p c j r", r=RUN),
+                in_=raw_of[(n, h)][:, :, share].rearrange("p j (c r) -> p c j r", r=RUN),
             )
             grouped_of[(n, h)] = grouped
 
-        def regroup_x2(n, h):
+        def regroup_on_gpsimd(n, h):
+            share = slice(VECTOR_COLUMNS, VECTOR_COLUMNS + GPSIMD_COLUMNS)
+            nc.gpsimd.tensor_scalar(
+                out=grouped_of[(n, h)][:, share, :],
+                in0=raw_of[(n, h)][:, :, share].rearrange("p j c -> p c j"),
+                scalar1=1.0,
+                scalar2=0.0,
+                op0=ALU.mult,
+                op1=ALU.add,
+            )
+
+        def regroup_on_scalar(n, h):
+            share = slice(COLUMNS - SCALAR_COLUMNS, COLUMNS)
             nc.scalar.copy(
-                out=grouped_of[(n, h)][:, 1].rearrange("p (c r) j -> p c j r", r=RUN),
-                in_=raw_of[(n, h)][:, 1].rearrange("p j (c r) -> p c j r", r=RUN),
+                out=grouped_of[(n, h)][:, share, :].rearrange("p (c r) j -> p c j r", r=RUN),
+                in_=raw_of[(n, h)][:, :, share].rearrange("p j (c r) -> p c j r", r=RUN),
             )
 
         def quantise(n, h):
@@ -123,7 +142,7 @@ def tile_fr_pa_t_kernel(
             nc.vector.quantize_mx(
                 out=codes[:].rearrange("p g w -> p (g w)").bitcast(FP8X4),
                 scales=planes[:].rearrange("p g w -> p (g w)"),
-                in_=grouped_of[(n, h)][:].rearrange("p g w j -> p (g w j)"),
+                in_=grouped_of[(n, h)][:].rearrange("p c j -> p (c j)"),
             )
             codes_of[(n, h)] = codes
             planes_of[(n, h)] = planes
@@ -186,7 +205,8 @@ def tile_fr_pa_t_kernel(
             front = t < BATCH
             back = t - 2
             if front:
-                regroup_x1(t, 0)
+                regroup_on_vector(t, 0)
+                regroup_on_gpsimd(t, 0)
             if 1 <= t <= BATCH:
                 quantise(t - 1, 1)
                 for i in range(HEADS):
@@ -195,15 +215,16 @@ def tile_fr_pa_t_kernel(
                 for i in range(HEADS):
                     first_exp(back, i)
             if front:
-                regroup_x2(t, 0)
+                regroup_on_scalar(t, 0)
             if back >= 0:
                 for i in range(HEADS):
                     top(back, i)
                 for i in range(HEADS):
                     second_exp(back, i)
             if front:
-                regroup_x1(t, 1)
-                regroup_x2(t, 1)
+                regroup_on_vector(t, 1)
+                regroup_on_gpsimd(t, 1)
+                regroup_on_scalar(t, 1)
                 quantise(t, 0)
             if back >= 0:
                 for i in range(HEADS):

@@ -193,10 +193,10 @@ def tile_fr_pa_t_kernel(
             for h in range(HALVES):
                 nc.vector.scalar_tensor_tensor(
                     out=e[:, h, :],
-                    in0=y_of[(n, i)][:, h, :],
-                    scalar=bias_of[i][:],
-                    in1=e[:, h, :],
-                    op0=ALU.add,
+                    in0=e[:, h, :],
+                    scalar=1.0,
+                    in1=y_of[(n, i)][:, h, :],
+                    op0=ALU.mult,
                     op1=ALU.mult,
                     accum_out=value_sum[:, i, n, h : h + 1],
                 )
@@ -204,13 +204,13 @@ def tile_fr_pa_t_kernel(
         for t in range(BATCH + 2):
             front = t < BATCH
             back = t - 2
-            if front:
-                regroup_on_vector(t, 0)
-                regroup_on_gpsimd(t, 0)
             if 1 <= t <= BATCH:
                 quantise(t - 1, 1)
                 for i in range(HEADS):
                     project(t - 1, i)
+            if front:
+                regroup_on_vector(t, 0)
+                regroup_on_gpsimd(t, 0)
             if back >= 0:
                 for i in range(HEADS):
                     first_exp(back, i)
@@ -222,10 +222,10 @@ def tile_fr_pa_t_kernel(
                 for i in range(HEADS):
                     second_exp(back, i)
             if front:
+                quantise(t, 0)
                 regroup_on_vector(t, 1)
                 regroup_on_gpsimd(t, 1)
                 regroup_on_scalar(t, 1)
-                quantise(t, 0)
             if back >= 0:
                 for i in range(HEADS):
                     weigh(back, i)
@@ -237,7 +237,13 @@ def tile_fr_pa_t_kernel(
         )
         inverse = keep.tile([P, columns], F32)
         nc.vector.reciprocal(out=inverse[:], in_=weight_sum[:].rearrange("p i n -> p (i n)"))
-        nc.vector.tensor_tensor(out=pooled[:, 0:columns], in0=value_total[:], in1=inverse[:], op=ALU.mult)
+        ratio = keep.tile([P, columns], F32)
+        nc.vector.tensor_tensor(out=ratio[:], in0=value_total[:], in1=inverse[:], op=ALU.mult)
+        for i in range(HEADS):
+            of_head = slice(i * BATCH, (i + 1) * BATCH)
+            nc.vector.tensor_scalar(
+                out=pooled[:, of_head], in0=ratio[:, of_head], scalar1=bias_of[i][:], scalar2=None, op0=ALU.add
+            )
         flipped = psum.tile([P, HALVES, HALF], F32, tag="y")
         nc.tensor.transpose(flipped[:, 0, 0:P], pooled[:], identity[:])
         rows_out = keep.tile([P, P], F32)

@@ -40,7 +40,7 @@ def tile_fr_pa_t_kernel(
 
     with ExitStack() as ctx:
         keep = ctx.enter_context(tc.tile_pool(name="keep", bufs=1))
-        group_pool = ctx.enter_context(tc.tile_pool(name="group", bufs=2))
+        group_pool = ctx.enter_context(tc.tile_pool(name="group", bufs=3))
         code_pool = ctx.enter_context(tc.tile_pool(name="code", bufs=4))
         soft_pool = ctx.enter_context(tc.tile_pool(name="soft", bufs=3))
         psum = ctx.enter_context(tc.psum_pool(name="psum", bufs=4))
@@ -109,14 +109,16 @@ def tile_fr_pa_t_kernel(
         weight_sum = keep.tile([P, HEADS, BATCH], F32)
         value_sum = keep.tile([P, HEADS, BATCH, HALVES], F32)
 
-        def regroup_on_vector(n, h):
+        def new_grouped(n, h):
             grouped = group_pool.tile([P, COLUMNS, PACK], BF16, align_bytes=64)
+            grouped_of[(n, h)] = grouped
+
+        def regroup_on_vector(n, h):
             share = slice(0, VECTOR_COLUMNS)
             nc.vector.tensor_copy(
-                out=grouped[:, share, :].rearrange("p (c r) j -> p c j r", r=RUN),
+                out=grouped_of[(n, h)][:, share, :].rearrange("p (c r) j -> p c j r", r=RUN),
                 in_=raw_of[(n, h)][:, :, share].rearrange("p j (c r) -> p c j r", r=RUN),
             )
-            grouped_of[(n, h)] = grouped
 
         def regroup_on_gpsimd(n, h):
             share = slice(VECTOR_COLUMNS, VECTOR_COLUMNS + GPSIMD_COLUMNS)
@@ -147,20 +149,20 @@ def tile_fr_pa_t_kernel(
             codes_of[(n, h)] = codes
             planes_of[(n, h)] = planes
 
-        def project(n, i):
-            y = psum.tile([P, HALVES, HALF], F32)
-            for h in range(HALVES):
-                for g in range(STREAMS):
-                    nc.tensor.matmul_mx(
-                        out=y[:, h, :],
-                        lhsT=w_codes[:, i, g, :].bitcast(FP8X4),
-                        lhsT_scale=w_planes[:, i, g, :],
-                        rhs=codes_of[(n, h)][:, g, :].bitcast(FP8X4),
-                        rhs_scale=planes_of[(n, h)][:, g, :],
-                        start=(g == 0),
-                        stop=(g == STREAMS - 1),
-                    )
-            y_of[(n, i)] = y
+        def project(n, h, i):
+            if h == 0:
+                y = psum.tile([P, HALVES, HALF], F32)
+                y_of[(n, i)] = y
+            for g in range(STREAMS):
+                nc.tensor.matmul_mx(
+                    out=y_of[(n, i)][:, h, :],
+                    lhsT=w_codes[:, i, g, :].bitcast(FP8X4),
+                    lhsT_scale=w_planes[:, i, g, :],
+                    rhs=codes_of[(n, h)][:, g, :].bitcast(FP8X4),
+                    rhs_scale=planes_of[(n, h)][:, g, :],
+                    start=(g == 0),
+                    stop=(g == STREAMS - 1),
+                )
 
         def first_exp(n, i):
             a = soft_pool.tile([P, HALVES, HALF], F32)
@@ -201,34 +203,36 @@ def tile_fr_pa_t_kernel(
                     accum_out=value_sum[:, i, n, h : h + 1],
                 )
 
-        for t in range(BATCH + 2):
-            front = t < BATCH
-            back = t - 2
-            if 1 <= t <= BATCH:
-                quantise(t - 1, 1)
+        units = BATCH * HALVES
+
+        def unit(u):
+            return divmod(u, HALVES)
+
+        for p in range(-3, units + 2):
+            if 0 <= p + 1 < units:
+                regroup_on_vector(*unit(p + 1))
+            if 0 <= p < units:
+                n, h = unit(p)
+                quantise(n, h)
                 for i in range(HEADS):
-                    project(t - 1, i)
-            if front:
-                regroup_on_vector(t, 0)
-                regroup_on_gpsimd(t, 0)
-            if back >= 0:
+                    project(n, h, i)
+            if 0 <= p + 3 < units:
+                new_grouped(*unit(p + 3))
+                regroup_on_gpsimd(*unit(p + 3))
+            back, second = divmod(p - 2, 2)
+            if 0 <= back < BATCH:
                 for i in range(HEADS):
-                    first_exp(back, i)
-            if front:
-                regroup_on_scalar(t, 0)
-            if back >= 0:
+                    if second:
+                        second_exp(back, i)
+                    else:
+                        first_exp(back, i)
                 for i in range(HEADS):
-                    top(back, i)
-                for i in range(HEADS):
-                    second_exp(back, i)
-            if front:
-                quantise(t, 0)
-                regroup_on_vector(t, 1)
-                regroup_on_gpsimd(t, 1)
-                regroup_on_scalar(t, 1)
-            if back >= 0:
-                for i in range(HEADS):
-                    weigh(back, i)
+                    if second:
+                        weigh(back, i)
+                    else:
+                        top(back, i)
+            if 0 <= p + 2 < units:
+                regroup_on_scalar(*unit(p + 2))
 
         columns = HEADS * BATCH
         value_total = keep.tile([P, columns], F32)

@@ -24,9 +24,9 @@ HEADS = 2
 OUT = 128
 RUN = 4
 COLUMNS = STREAMS * HALF
-VECTOR_COLUMNS = 320
-GPSIMD_COLUMNS = 256
-SCALAR_COLUMNS = COLUMNS - VECTOR_COLUMNS - GPSIMD_COLUMNS
+HELPER_COLUMNS = 576
+SCALAR_COLUMNS = COLUMNS - HELPER_COLUMNS
+VECTOR_UNITS = 3
 
 FLOPS = 2 * BATCH * HEADS * OUT * STREAMS * P * PACK * POSITIONS
 
@@ -114,14 +114,14 @@ def tile_fr_pa_t_kernel(
             grouped_of[(n, h)] = grouped
 
         def regroup_on_vector(n, h):
-            share = slice(0, VECTOR_COLUMNS)
+            share = slice(0, HELPER_COLUMNS)
             nc.vector.tensor_copy(
                 out=grouped_of[(n, h)][:, share, :].rearrange("p (c r) j -> p c j r", r=RUN),
                 in_=raw_of[(n, h)][:, :, share].rearrange("p j (c r) -> p c j r", r=RUN),
             )
 
         def regroup_on_gpsimd(n, h):
-            share = slice(VECTOR_COLUMNS, VECTOR_COLUMNS + GPSIMD_COLUMNS)
+            share = slice(0, HELPER_COLUMNS)
             nc.gpsimd.tensor_scalar(
                 out=grouped_of[(n, h)][:, share, :],
                 in0=raw_of[(n, h)][:, :, share].rearrange("p j c -> p c j"),
@@ -209,7 +209,7 @@ def tile_fr_pa_t_kernel(
             return divmod(u, HALVES)
 
         for p in range(-3, units + 2):
-            if 0 <= p + 1 < units:
+            if 0 <= p + 1 < VECTOR_UNITS:
                 regroup_on_vector(*unit(p + 1))
             if 0 <= p < units:
                 n, h = unit(p)
@@ -218,7 +218,8 @@ def tile_fr_pa_t_kernel(
                     project(n, h, i)
             if 0 <= p + 3 < units:
                 new_grouped(*unit(p + 3))
-                regroup_on_gpsimd(*unit(p + 3))
+                if p + 3 >= VECTOR_UNITS:
+                    regroup_on_gpsimd(*unit(p + 3))
             back, second = divmod(p - 2, 2)
             if 0 <= back < BATCH:
                 for i in range(HEADS):

@@ -10,6 +10,7 @@ U32 = mybir.dt.uint32
 U8 = mybir.dt.uint8
 I32 = mybir.dt.int32
 EXP = mybir.ActivationFunctionType.Exp
+COPY = mybir.ActivationFunctionType.Copy
 ALU = mybir.AluOpType
 AXIS_X = mybir.AxisListType.X
 
@@ -24,8 +25,8 @@ HEADS = 2
 OUT = 128
 RUN = 4
 COLUMNS = STREAMS * HALF
-HELPER_COLUMNS = 576
-SCALAR_COLUMNS = COLUMNS - HELPER_COLUMNS
+SCALAR_COLUMNS = 448
+EARLY_SCALAR_COLUMNS = 256
 VECTOR_UNITS = 3
 
 FLOPS = 2 * BATCH * HEADS * OUT * STREAMS * P * PACK * POSITIONS
@@ -74,27 +75,27 @@ def tile_fr_pa_t_kernel(
         def load_bias(i):
             words, scales, b = weights[i]
             bias = keep.tile([P, 1], BF16, name="bias_%d" % i)
-            nc.sync.dma_start(out=bias[:], in_=b.rearrange("(o one) -> o one", one=1))
+            nc.gpsimd.dma_start(out=bias[:], in_=b.rearrange("(o one) -> o one", one=1))
             bias_of[i] = bias
 
-        def load_x(n, h):
-            raw = keep.tile([P, PACK, COLUMNS], BF16, name="raw_%d_%d" % (n, h))
-            for g, x in enumerate(streams):
-                rows = x[n].rearrange("(p j) a b -> p j (a b)", j=PACK)
-                nc.sync.dma_start(
-                    out=raw[:, :, g * HALF : (g + 1) * HALF], in_=rows[:, :, h * HALF : (h + 1) * HALF]
-                )
-            raw_of[(n, h)] = raw
+        def load_x(n, h, g):
+            if g == 0:
+                raw = keep.tile([P, PACK, COLUMNS], BF16, name="raw_%d_%d" % (n, h))
+                raw_of[(n, h)] = raw
+            rows = streams[g][n].rearrange("(p j) a b -> p j (a b)", j=PACK)
+            nc.sync.dma_start(
+                out=raw_of[(n, h)][:, :, g * HALF : (g + 1) * HALF], in_=rows[:, :, h * HALF : (h + 1) * HALF]
+            )
 
-        load_weight(0)
-        load_x(0, 0)
-        load_weight(1)
-        load_x(0, 1)
+        big = [(n, h, g) for n in range(BATCH) for h in range(HALVES) for g in range(STREAMS)]
+        for place, load in enumerate(big):
+            if place == 2:
+                load_weight(0)
+            if place == 5:
+                load_weight(1)
+            load_x(*load)
         load_bias(0)
         load_bias(1)
-        for n in range(1, BATCH):
-            for h in range(HALVES):
-                load_x(n, h)
 
         warm = keep.tile([P, 1], F32)
         nc.vector.memset(warm[:], 0.0)
@@ -102,26 +103,30 @@ def tile_fr_pa_t_kernel(
 
         identity = keep.tile([P, P], F32)
         make_identity(nc, identity[:])
-        pooled = keep.tile([P, P], F32)
-        nc.gpsimd.memset(pooled[:], 0.0)
-
         neg_top = keep.tile([P, HEADS, BATCH], F32)
-        weight_sum = keep.tile([P, HEADS, BATCH], F32)
-        value_sum = keep.tile([P, HEADS, BATCH, HALVES], F32)
+        weight_sum = keep.tile([P, P], F32)
+        nc.gpsimd.memset(weight_sum[:], 1.0)
+        value_sum = keep.tile([P, HALVES, P], F32)
+        nc.gpsimd.memset(value_sum[:].rearrange("p h c -> p (h c)"), 0.0)
+        bias_sum = keep.tile([P, P], F32)
+        nc.gpsimd.memset(bias_sum[:], 0.0)
+        bias_f32 = keep.tile([P, HEADS], F32)
+        for i in range(HEADS):
+            nc.gpsimd.tensor_copy(out=bias_f32[:, i : i + 1], in_=bias_of[i][:])
 
         def new_grouped(n, h):
             grouped = group_pool.tile([P, COLUMNS, PACK], BF16, align_bytes=64)
             grouped_of[(n, h)] = grouped
 
         def regroup_on_vector(n, h):
-            share = slice(0, HELPER_COLUMNS)
+            share = slice(EARLY_SCALAR_COLUMNS, COLUMNS)
             nc.vector.tensor_copy(
                 out=grouped_of[(n, h)][:, share, :].rearrange("p (c r) j -> p c j r", r=RUN),
                 in_=raw_of[(n, h)][:, :, share].rearrange("p j (c r) -> p c j r", r=RUN),
             )
 
         def regroup_on_gpsimd(n, h):
-            share = slice(0, HELPER_COLUMNS)
+            share = slice(SCALAR_COLUMNS, COLUMNS)
             nc.gpsimd.tensor_scalar(
                 out=grouped_of[(n, h)][:, share, :],
                 in0=raw_of[(n, h)][:, :, share].rearrange("p j c -> p c j"),
@@ -132,7 +137,7 @@ def tile_fr_pa_t_kernel(
             )
 
         def regroup_on_scalar(n, h):
-            share = slice(COLUMNS - SCALAR_COLUMNS, COLUMNS)
+            share = slice(0, EARLY_SCALAR_COLUMNS if HALVES * n + h < VECTOR_UNITS else SCALAR_COLUMNS)
             nc.scalar.copy(
                 out=grouped_of[(n, h)][:, share, :].rearrange("p (c r) j -> p c j r", r=RUN),
                 in_=raw_of[(n, h)][:, :, share].rearrange("p j (c r) -> p c j r", r=RUN),
@@ -186,7 +191,7 @@ def tile_fr_pa_t_kernel(
                 in_=a_of[(n, i)][:].rearrange("p h w -> p (h w)"),
                 func=EXP,
                 bias=neg_top[:, i, n : n + 1],
-                accum_out=weight_sum[:, i, n : n + 1],
+                accum_out=weight_sum[:, BATCH * i + n : BATCH * i + n + 1],
             )
             e_of[(n, i)] = e
 
@@ -200,7 +205,7 @@ def tile_fr_pa_t_kernel(
                     in1=y_of[(n, i)][:, h, :],
                     op0=ALU.mult,
                     op1=ALU.mult,
-                    accum_out=value_sum[:, i, n, h : h + 1],
+                    accum_out=value_sum[:, h, BATCH * i + n : BATCH * i + n + 1],
                 )
 
         units = BATCH * HALVES
@@ -209,13 +214,13 @@ def tile_fr_pa_t_kernel(
             return divmod(u, HALVES)
 
         for p in range(-3, units + 2):
-            if 0 <= p + 1 < VECTOR_UNITS:
-                regroup_on_vector(*unit(p + 1))
             if 0 <= p < units:
                 n, h = unit(p)
                 quantise(n, h)
                 for i in range(HEADS):
                     project(n, h, i)
+            if 0 <= p + 1 < VECTOR_UNITS:
+                regroup_on_vector(*unit(p + 1))
             if 0 <= p + 3 < units:
                 new_grouped(*unit(p + 3))
                 if p + 3 >= VECTOR_UNITS:
@@ -235,23 +240,27 @@ def tile_fr_pa_t_kernel(
             if 0 <= p + 2 < units:
                 regroup_on_scalar(*unit(p + 2))
 
-        columns = HEADS * BATCH
-        value_total = keep.tile([P, columns], F32)
-        nc.vector.tensor_reduce(
-            out=value_total[:], in_=value_sum[:].rearrange("p i n h -> p (i n) h"), axis=AXIS_X, op=ALU.add
-        )
-        inverse = keep.tile([P, columns], F32)
-        nc.vector.reciprocal(out=inverse[:], in_=weight_sum[:].rearrange("p i n -> p (i n)"))
-        ratio = keep.tile([P, columns], F32)
-        nc.vector.tensor_tensor(out=ratio[:], in0=value_total[:], in1=inverse[:], op=ALU.mult)
         for i in range(HEADS):
-            of_head = slice(i * BATCH, (i + 1) * BATCH)
-            nc.vector.tensor_scalar(
-                out=pooled[:, of_head], in0=ratio[:, of_head], scalar1=bias_of[i][:], scalar2=None, op0=ALU.add
+            of_head = slice(BATCH * i, BATCH * (i + 1))
+            nc.scalar.activation(
+                out=bias_sum[:, of_head], in_=weight_sum[:, of_head], func=COPY, scale=bias_f32[:, i : i + 1]
             )
+        flipped_weight = psum.tile([P, HALVES, HALF], F32, tag="y")
+        nc.tensor.transpose(flipped_weight[:, 0, 0:P], weight_sum[:], identity[:])
+        inverse = keep.tile([P, P], F32)
+        nc.vector.reciprocal(out=inverse[:], in_=flipped_weight[:, 0, 0:P])
         flipped = psum.tile([P, HALVES, HALF], F32, tag="y")
-        nc.tensor.transpose(flipped[:, 0, 0:P], pooled[:], identity[:])
+        terms = [bias_sum[:]] + [value_sum[:, h, :] for h in range(HALVES)]
+        for k, term in enumerate(terms):
+            nc.tensor.matmul(
+                out=flipped[:, 0, 0:P],
+                lhsT=term,
+                rhs=identity[:],
+                is_transpose=True,
+                start=(k == 0),
+                stop=(k == len(terms) - 1),
+            )
         rows_out = keep.tile([P, P], F32)
-        nc.vector.tensor_copy(out=rows_out[:], in_=flipped[:, 0, 0:P])
+        nc.vector.tensor_tensor(out=rows_out[:], in0=flipped[:, 0, 0:P], in1=inverse[:], op=ALU.mult)
         nc.sync.dma_start(out=out_0, in_=rows_out[0:BATCH, :])
-        nc.sync.dma_start(out=out_1, in_=rows_out[BATCH : 2 * BATCH, :])
+        nc.scalar.dma_start(out=out_1, in_=rows_out[BATCH : 2 * BATCH, :])

@@ -25,9 +25,11 @@ HEADS = 2
 OUT = 128
 RUN = 4
 COLUMNS = STREAMS * HALF
-SCALAR_COLUMNS = 448
-EARLY_SCALAR_COLUMNS = 256
+STAGED_COLUMNS = 192
+SCALAR_COLUMNS = 320
+EARLY_SCALAR_COLUMNS = 192
 VECTOR_UNITS = 3
+MATMUL_COLUMNS = 128
 
 FLOPS = 2 * BATCH * HEADS * OUT * STREAMS * P * PACK * POSITIONS
 
@@ -44,11 +46,13 @@ def tile_fr_pa_t_kernel(
         group_pool = ctx.enter_context(tc.tile_pool(name="group", bufs=3))
         code_pool = ctx.enter_context(tc.tile_pool(name="code", bufs=4))
         soft_pool = ctx.enter_context(tc.tile_pool(name="soft", bufs=3))
-        psum = ctx.enter_context(tc.psum_pool(name="psum", bufs=4))
+        psum = ctx.enter_context(tc.psum_pool(name="psum", bufs=3))
+        stage_pool = ctx.enter_context(tc.psum_pool(name="stage", bufs=2))
         ctx.enter_context(tc.manual_schedule())
 
         raw_of = {}
         grouped_of = {}
+        staged_of = {}
         codes_of = {}
         planes_of = {}
         y_of = {}
@@ -103,6 +107,8 @@ def tile_fr_pa_t_kernel(
 
         identity = keep.tile([P, P], F32)
         make_identity(nc, identity[:])
+        identity_bf16 = keep.tile([P, P], BF16)
+        make_identity(nc, identity_bf16[:])
         neg_top = keep.tile([P, HEADS, BATCH], F32)
         weight_sum = keep.tile([P, P], F32)
         nc.gpsimd.memset(weight_sum[:], 1.0)
@@ -119,14 +125,14 @@ def tile_fr_pa_t_kernel(
             grouped_of[(n, h)] = grouped
 
         def regroup_on_vector(n, h):
-            share = slice(EARLY_SCALAR_COLUMNS, COLUMNS)
+            share = slice(STAGED_COLUMNS + EARLY_SCALAR_COLUMNS, COLUMNS)
             nc.vector.tensor_copy(
                 out=grouped_of[(n, h)][:, share, :].rearrange("p (c r) j -> p c j r", r=RUN),
                 in_=raw_of[(n, h)][:, :, share].rearrange("p j (c r) -> p c j r", r=RUN),
             )
 
         def regroup_on_gpsimd(n, h):
-            share = slice(SCALAR_COLUMNS, COLUMNS)
+            share = slice(STAGED_COLUMNS + SCALAR_COLUMNS, COLUMNS)
             nc.gpsimd.tensor_scalar(
                 out=grouped_of[(n, h)][:, share, :],
                 in0=raw_of[(n, h)][:, :, share].rearrange("p j c -> p c j"),
@@ -136,8 +142,28 @@ def tile_fr_pa_t_kernel(
                 op1=ALU.add,
             )
 
+        def stage_on_tensor(n, h):
+            staged = stage_pool.tile([P, 2 * HALF], BF16)
+            for first in range(0, STAGED_COLUMNS, MATMUL_COLUMNS):
+                share = slice(first, min(first + MATMUL_COLUMNS, STAGED_COLUMNS))
+                nc.tensor.matmul(
+                    out=staged[:, PACK * share.start : PACK * share.stop].rearrange("p (c j) -> p c j", j=PACK),
+                    lhsT=identity_bf16[:],
+                    rhs=raw_of[(n, h)][:, :, share].rearrange("p j c -> p c j"),
+                    start=True,
+                    stop=True,
+                )
+            staged_of[(n, h)] = staged
+
+        def unstage_on_scalar(n, h):
+            nc.scalar.copy(
+                out=grouped_of[(n, h)][:, 0:STAGED_COLUMNS, :].rearrange("p c j -> p (c j)"),
+                in_=staged_of[(n, h)][:, 0 : PACK * STAGED_COLUMNS],
+            )
+
         def regroup_on_scalar(n, h):
-            share = slice(0, EARLY_SCALAR_COLUMNS if HALVES * n + h < VECTOR_UNITS else SCALAR_COLUMNS)
+            own = EARLY_SCALAR_COLUMNS if HALVES * n + h < VECTOR_UNITS else SCALAR_COLUMNS
+            share = slice(STAGED_COLUMNS, STAGED_COLUMNS + own)
             nc.scalar.copy(
                 out=grouped_of[(n, h)][:, share, :].rearrange("p (c r) j -> p c j r", r=RUN),
                 in_=raw_of[(n, h)][:, :, share].rearrange("p j (c r) -> p c j r", r=RUN),
@@ -214,11 +240,12 @@ def tile_fr_pa_t_kernel(
             return divmod(u, HALVES)
 
         for p in range(-3, units + 2):
+            if 0 <= p + 2 < units:
+                stage_on_tensor(*unit(p + 2))
             if 0 <= p < units:
                 n, h = unit(p)
                 quantise(n, h)
-                for i in range(HEADS):
-                    project(n, h, i)
+                project(n, h, 0)
             if 0 <= p + 1 < VECTOR_UNITS:
                 regroup_on_vector(*unit(p + 1))
             if 0 <= p + 3 < units:
@@ -232,12 +259,18 @@ def tile_fr_pa_t_kernel(
                         second_exp(back, i)
                     else:
                         first_exp(back, i)
+            if 0 <= back < BATCH and second:
+                weigh(back, 0)
+            if 0 <= p < units and p % HALVES == HALVES - 1:
+                for h in range(HALVES):
+                    project(p // HALVES, h, 1)
+            if 0 <= back < BATCH and second:
+                weigh(back, 1)
+            if 0 <= back < BATCH and not second:
                 for i in range(HEADS):
-                    if second:
-                        weigh(back, i)
-                    else:
-                        top(back, i)
+                    top(back, i)
             if 0 <= p + 2 < units:
+                unstage_on_scalar(*unit(p + 2))
                 regroup_on_scalar(*unit(p + 2))
 
         for i in range(HEADS):

@@ -29,6 +29,7 @@ STAGED_COLUMNS = 192
 SCALAR_COLUMNS = 320
 EARLY_SCALAR_COLUMNS = 192
 VECTOR_UNITS = 3
+VECTOR_UNSTAGES = range(4, 14, 2)
 MATMUL_COLUMNS = 128
 
 FLOPS = 2 * BATCH * HEADS * OUT * STREAMS * P * PACK * POSITIONS
@@ -142,6 +143,9 @@ def tile_fr_pa_t_kernel(
                 op1=ALU.add,
             )
 
+        def gate_gpsimd(n, h):
+            nc.vector.memset(grouped_of[(n, h)][:, COLUMNS - 1, 0:1], 1.0)
+
         def stage_on_tensor(n, h):
             staged = stage_pool.tile([P, 2 * HALF], BF16)
             for first in range(0, STAGED_COLUMNS, MATMUL_COLUMNS):
@@ -157,6 +161,12 @@ def tile_fr_pa_t_kernel(
 
         def unstage_on_scalar(n, h):
             nc.scalar.copy(
+                out=grouped_of[(n, h)][:, 0:STAGED_COLUMNS, :].rearrange("p c j -> p (c j)"),
+                in_=staged_of[(n, h)][:, 0 : PACK * STAGED_COLUMNS],
+            )
+
+        def unstage_on_vector(n, h):
+            nc.vector.tensor_copy(
                 out=grouped_of[(n, h)][:, 0:STAGED_COLUMNS, :].rearrange("p c j -> p (c j)"),
                 in_=staged_of[(n, h)][:, 0 : PACK * STAGED_COLUMNS],
             )
@@ -242,16 +252,18 @@ def tile_fr_pa_t_kernel(
         for p in range(-3, units + 2):
             if 0 <= p + 2 < units:
                 stage_on_tensor(*unit(p + 2))
+            if VECTOR_UNITS <= p + 2 < units:
+                gate_gpsimd(*unit(p + 2))
             if 0 <= p < units:
                 n, h = unit(p)
                 quantise(n, h)
                 project(n, h, 0)
             if 0 <= p + 1 < VECTOR_UNITS:
                 regroup_on_vector(*unit(p + 1))
+            if VECTOR_UNITS <= p + 2 < units:
+                regroup_on_gpsimd(*unit(p + 2))
             if 0 <= p + 3 < units:
                 new_grouped(*unit(p + 3))
-                if p + 3 >= VECTOR_UNITS:
-                    regroup_on_gpsimd(*unit(p + 3))
             back, second = divmod(p - 2, 2)
             if 0 <= back < BATCH:
                 for i in range(HEADS):
@@ -270,7 +282,10 @@ def tile_fr_pa_t_kernel(
                 for i in range(HEADS):
                     top(back, i)
             if 0 <= p + 2 < units:
-                unstage_on_scalar(*unit(p + 2))
+                if p + 2 in VECTOR_UNSTAGES:
+                    unstage_on_vector(*unit(p + 2))
+                else:
+                    unstage_on_scalar(*unit(p + 2))
                 regroup_on_scalar(*unit(p + 2))
 
         for i in range(HEADS):

@@ -25,11 +25,13 @@ HEADS = 2
 OUT = 128
 RUN = 4
 COLUMNS = STREAMS * HALF
-STAGED_COLUMNS = 192
-SCALAR_COLUMNS = 320
-EARLY_SCALAR_COLUMNS = 192
-VECTOR_UNITS = 3
-VECTOR_UNSTAGES = range(4, 14, 2)
+PRODUCT_COLUMNS = 2 * HALF // PACK
+STAGED_COLUMNS = 204
+SCALAR_COLUMNS = 324
+EARLY_SCALAR_COLUMNS = 188
+VECTOR_UNITS = 4
+FIRST_VECTOR_UNSTAGE = 5
+OVERLAP = 1
 MATMUL_COLUMNS = 128
 
 FLOPS = 2 * BATCH * HEADS * OUT * STREAMS * P * PACK * POSITIONS
@@ -94,11 +96,13 @@ def tile_fr_pa_t_kernel(
 
         big = [(n, h, g) for n in range(BATCH) for h in range(HALVES) for g in range(STREAMS)]
         for place, load in enumerate(big):
-            if place == 2:
+            if place == 4:
                 load_weight(0)
-            if place == 5:
+            if place == 8:
                 load_weight(1)
             load_x(*load)
+        identity_bf16 = keep.tile([P, P], BF16)
+        make_identity(nc, identity_bf16[:])
         load_bias(0)
         load_bias(1)
 
@@ -108,8 +112,6 @@ def tile_fr_pa_t_kernel(
 
         identity = keep.tile([P, P], F32)
         make_identity(nc, identity[:])
-        identity_bf16 = keep.tile([P, P], BF16)
-        make_identity(nc, identity_bf16[:])
         neg_top = keep.tile([P, HEADS, BATCH], F32)
         weight_sum = keep.tile([P, P], F32)
         nc.gpsimd.memset(weight_sum[:], 1.0)
@@ -125,15 +127,28 @@ def tile_fr_pa_t_kernel(
             grouped = group_pool.tile([P, COLUMNS, PACK], BF16, align_bytes=64)
             grouped_of[(n, h)] = grouped
 
+        def scalar_columns(n, h):
+            return EARLY_SCALAR_COLUMNS if HALVES * n + h < VECTOR_UNITS else SCALAR_COLUMNS
+
+        def vector_unstages(n, h):
+            return HALVES * n + h >= FIRST_VECTOR_UNSTAGE and h == 1
+
+        def helper_share(n, h):
+            return slice(scalar_columns(n, h) + STAGED_COLUMNS, COLUMNS)
+
+        def staged_share(n, h):
+            first = scalar_columns(n, h)
+            return slice(first, first + STAGED_COLUMNS + (OVERLAP if vector_unstages(n, h) else 0))
+
         def regroup_on_vector(n, h):
-            share = slice(STAGED_COLUMNS + EARLY_SCALAR_COLUMNS, COLUMNS)
+            share = helper_share(n, h)
             nc.vector.tensor_copy(
                 out=grouped_of[(n, h)][:, share, :].rearrange("p (c r) j -> p c j r", r=RUN),
                 in_=raw_of[(n, h)][:, :, share].rearrange("p j (c r) -> p c j r", r=RUN),
             )
 
         def regroup_on_gpsimd(n, h):
-            share = slice(STAGED_COLUMNS + SCALAR_COLUMNS, COLUMNS)
+            share = helper_share(n, h)
             nc.gpsimd.tensor_scalar(
                 out=grouped_of[(n, h)][:, share, :],
                 in0=raw_of[(n, h)][:, :, share].rearrange("p j c -> p c j"),
@@ -143,15 +158,14 @@ def tile_fr_pa_t_kernel(
                 op1=ALU.add,
             )
 
-        def gate_gpsimd(n, h):
-            nc.vector.memset(grouped_of[(n, h)][:, COLUMNS - 1, 0:1], 1.0)
-
         def stage_on_tensor(n, h):
             staged = stage_pool.tile([P, 2 * HALF], BF16)
-            for first in range(0, STAGED_COLUMNS, MATMUL_COLUMNS):
-                share = slice(first, min(first + MATMUL_COLUMNS, STAGED_COLUMNS))
+            of = staged_share(n, h)
+            for first in range(of.start, of.stop, MATMUL_COLUMNS):
+                share = slice(first, min(first + MATMUL_COLUMNS, of.stop))
+                into = slice(PACK * (share.start - of.start), PACK * (share.stop - of.start))
                 nc.tensor.matmul(
-                    out=staged[:, PACK * share.start : PACK * share.stop].rearrange("p (c j) -> p c j", j=PACK),
+                    out=staged[:, into].rearrange("p (c j) -> p c j", j=PACK),
                     lhsT=identity_bf16[:],
                     rhs=raw_of[(n, h)][:, :, share].rearrange("p j c -> p c j"),
                     start=True,
@@ -159,21 +173,15 @@ def tile_fr_pa_t_kernel(
                 )
             staged_of[(n, h)] = staged
 
-        def unstage_on_scalar(n, h):
-            nc.scalar.copy(
-                out=grouped_of[(n, h)][:, 0:STAGED_COLUMNS, :].rearrange("p c j -> p (c j)"),
-                in_=staged_of[(n, h)][:, 0 : PACK * STAGED_COLUMNS],
-            )
-
-        def unstage_on_vector(n, h):
-            nc.vector.tensor_copy(
-                out=grouped_of[(n, h)][:, 0:STAGED_COLUMNS, :].rearrange("p c j -> p (c j)"),
-                in_=staged_of[(n, h)][:, 0 : PACK * STAGED_COLUMNS],
+        def unstage(copy, n, h):
+            of = staged_share(n, h)
+            copy(
+                out=grouped_of[(n, h)][:, of, :].rearrange("p c j -> p (c j)"),
+                in_=staged_of[(n, h)][:, 0 : PACK * (of.stop - of.start)],
             )
 
         def regroup_on_scalar(n, h):
-            own = EARLY_SCALAR_COLUMNS if HALVES * n + h < VECTOR_UNITS else SCALAR_COLUMNS
-            share = slice(STAGED_COLUMNS, STAGED_COLUMNS + own)
+            share = slice(0, scalar_columns(n, h))
             nc.scalar.copy(
                 out=grouped_of[(n, h)][:, share, :].rearrange("p (c r) j -> p c j r", r=RUN),
                 in_=raw_of[(n, h)][:, :, share].rearrange("p j (c r) -> p c j r", r=RUN),
@@ -231,11 +239,15 @@ def tile_fr_pa_t_kernel(
             )
             e_of[(n, i)] = e
 
-        def weigh(n, i):
+        def weigh(n, i, gated=None):
             e = e_of[(n, i)]
             for h in range(HALVES):
+                products = e[:, h, :]
+                if h == HALVES - 1 and gated is not None:
+                    place = grouped_of[gated][:, COLUMNS - PRODUCT_COLUMNS : COLUMNS, :]
+                    products = place.rearrange("p c j -> p (c j)").bitcast(F32)
                 nc.vector.scalar_tensor_tensor(
-                    out=e[:, h, :],
+                    out=products,
                     in0=e[:, h, :],
                     scalar=1.0,
                     in1=y_of[(n, i)][:, h, :],
@@ -250,20 +262,19 @@ def tile_fr_pa_t_kernel(
             return divmod(u, HALVES)
 
         for p in range(-3, units + 2):
-            if 0 <= p + 2 < units:
-                stage_on_tensor(*unit(p + 2))
-            if VECTOR_UNITS <= p + 2 < units:
-                gate_gpsimd(*unit(p + 2))
+            for u in (p + 2, p + 3):
+                if 0 <= u < units and (u == p + 3) == (u >= FIRST_VECTOR_UNSTAGE):
+                    stage_on_tensor(*unit(u))
             if 0 <= p < units:
                 n, h = unit(p)
                 quantise(n, h)
                 project(n, h, 0)
             if 0 <= p + 1 < VECTOR_UNITS:
                 regroup_on_vector(*unit(p + 1))
-            if VECTOR_UNITS <= p + 2 < units:
-                regroup_on_gpsimd(*unit(p + 2))
             if 0 <= p + 3 < units:
                 new_grouped(*unit(p + 3))
+            if VECTOR_UNITS <= p + 3 < FIRST_VECTOR_UNSTAGE:
+                regroup_on_gpsimd(*unit(p + 3))
             back, second = divmod(p - 2, 2)
             if 0 <= back < BATCH:
                 for i in range(HEADS):
@@ -277,16 +288,18 @@ def tile_fr_pa_t_kernel(
                 for h in range(HALVES):
                     project(p // HALVES, h, 1)
             if 0 <= back < BATCH and second:
-                weigh(back, 1)
+                weigh(back, 1, gated=unit(p + 3) if p + 3 < units else None)
             if 0 <= back < BATCH and not second:
                 for i in range(HEADS):
                     top(back, i)
+            if 0 <= p + 3 < units and vector_unstages(*unit(p + 3)):
+                unstage(nc.vector.tensor_copy, *unit(p + 3))
+            if FIRST_VECTOR_UNSTAGE <= p + 3 < units:
+                regroup_on_gpsimd(*unit(p + 3))
             if 0 <= p + 2 < units:
-                if p + 2 in VECTOR_UNSTAGES:
-                    unstage_on_vector(*unit(p + 2))
-                else:
-                    unstage_on_scalar(*unit(p + 2))
                 regroup_on_scalar(*unit(p + 2))
+                if not vector_unstages(*unit(p + 2)):
+                    unstage(nc.scalar.copy, *unit(p + 2))
 
         for i in range(HEADS):
             of_head = slice(BATCH * i, BATCH * (i + 1))

@@ -24,7 +24,7 @@ HALVES = POSITIONS // HALF
 HEADS = 2
 OUT = 128
 RUN = 4
-COLUMNS = STREAMS * HALF
+COLUMNS = POSITIONS
 PRODUCT_COLUMNS = 2 * HALF // PACK
 STAGED_COLUMNS = 204
 SCALAR_COLUMNS = 324
@@ -85,22 +85,22 @@ def tile_fr_pa_t_kernel(
             nc.gpsimd.dma_start(out=bias[:], in_=b.rearrange("(o one) -> o one", one=1))
             bias_of[i] = bias
 
-        def load_x(n, h, g):
-            if g == 0:
-                raw = keep.tile([P, PACK, COLUMNS], BF16, name="raw_%d_%d" % (n, h))
-                raw_of[(n, h)] = raw
+        def load_x(n, g, columns):
+            if columns.start == 0:
+                raw = keep.tile([P, PACK, COLUMNS], BF16, name="raw_%d_%d" % (n, g))
+                raw_of[(n, g)] = raw
             rows = streams[g][n].rearrange("(p j) a b -> p j (a b)", j=PACK)
-            nc.sync.dma_start(
-                out=raw_of[(n, h)][:, :, g * HALF : (g + 1) * HALF], in_=rows[:, :, h * HALF : (h + 1) * HALF]
-            )
+            nc.sync.dma_start(out=raw_of[(n, g)][:, :, columns], in_=rows[:, :, columns])
 
-        big = [(n, h, g) for n in range(BATCH) for h in range(HALVES) for g in range(STREAMS)]
-        for place, load in enumerate(big):
-            if place == 4:
+        for u in range(BATCH * STREAMS):
+            n, g = divmod(u, STREAMS)
+            pieces = HALVES if u == 0 else 1
+            for k in range(pieces):
+                load_x(n, g, slice(k * COLUMNS // pieces, (k + 1) * COLUMNS // pieces))
+            if u == 0:
                 load_weight(0)
-            if place == 8:
+            if u == 1:
                 load_weight(1)
-            load_x(*load)
         identity_bf16 = keep.tile([P, P], BF16)
         make_identity(nc, identity_bf16[:])
         load_bias(0)
@@ -123,95 +123,95 @@ def tile_fr_pa_t_kernel(
         for i in range(HEADS):
             nc.gpsimd.tensor_copy(out=bias_f32[:, i : i + 1], in_=bias_of[i][:])
 
-        def new_grouped(n, h):
+        def new_grouped(n, g):
             grouped = group_pool.tile([P, COLUMNS, PACK], BF16, align_bytes=64)
-            grouped_of[(n, h)] = grouped
+            grouped_of[(n, g)] = grouped
 
-        def scalar_columns(n, h):
-            return EARLY_SCALAR_COLUMNS if HALVES * n + h < VECTOR_UNITS else SCALAR_COLUMNS
+        def scalar_columns(n, g):
+            return EARLY_SCALAR_COLUMNS if STREAMS * n + g < VECTOR_UNITS else SCALAR_COLUMNS
 
-        def vector_unstages(n, h):
-            return HALVES * n + h >= FIRST_VECTOR_UNSTAGE and h == 1
+        def vector_unstages(n, g):
+            return STREAMS * n + g >= FIRST_VECTOR_UNSTAGE and g == 1
 
-        def helper_share(n, h):
-            return slice(scalar_columns(n, h) + STAGED_COLUMNS, COLUMNS)
+        def helper_share(n, g):
+            return slice(scalar_columns(n, g) + STAGED_COLUMNS, COLUMNS)
 
-        def staged_share(n, h):
-            first = scalar_columns(n, h)
-            return slice(first, first + STAGED_COLUMNS + (OVERLAP if vector_unstages(n, h) else 0))
+        def staged_share(n, g):
+            first = scalar_columns(n, g)
+            return slice(first, first + STAGED_COLUMNS + (OVERLAP if vector_unstages(n, g) else 0))
 
-        def regroup_on_vector(n, h):
-            share = helper_share(n, h)
+        def regroup_on_vector(n, g):
+            share = helper_share(n, g)
             nc.vector.tensor_copy(
-                out=grouped_of[(n, h)][:, share, :].rearrange("p (c r) j -> p c j r", r=RUN),
-                in_=raw_of[(n, h)][:, :, share].rearrange("p j (c r) -> p c j r", r=RUN),
+                out=grouped_of[(n, g)][:, share, :].rearrange("p (c r) j -> p c j r", r=RUN),
+                in_=raw_of[(n, g)][:, :, share].rearrange("p j (c r) -> p c j r", r=RUN),
             )
 
-        def regroup_on_gpsimd(n, h):
-            share = helper_share(n, h)
+        def regroup_on_gpsimd(n, g):
+            share = helper_share(n, g)
             nc.gpsimd.tensor_scalar(
-                out=grouped_of[(n, h)][:, share, :],
-                in0=raw_of[(n, h)][:, :, share].rearrange("p j c -> p c j"),
+                out=grouped_of[(n, g)][:, share, :],
+                in0=raw_of[(n, g)][:, :, share].rearrange("p j c -> p c j"),
                 scalar1=1.0,
                 scalar2=0.0,
                 op0=ALU.mult,
                 op1=ALU.add,
             )
 
-        def stage_on_tensor(n, h):
+        def stage_on_tensor(n, g):
             staged = stage_pool.tile([P, 2 * HALF], BF16)
-            of = staged_share(n, h)
+            of = staged_share(n, g)
             for first in range(of.start, of.stop, MATMUL_COLUMNS):
                 share = slice(first, min(first + MATMUL_COLUMNS, of.stop))
                 into = slice(PACK * (share.start - of.start), PACK * (share.stop - of.start))
                 nc.tensor.matmul(
                     out=staged[:, into].rearrange("p (c j) -> p c j", j=PACK),
                     lhsT=identity_bf16[:],
-                    rhs=raw_of[(n, h)][:, :, share].rearrange("p j c -> p c j"),
+                    rhs=raw_of[(n, g)][:, :, share].rearrange("p j c -> p c j"),
                     start=True,
                     stop=True,
                 )
-            staged_of[(n, h)] = staged
+            staged_of[(n, g)] = staged
 
-        def unstage(copy, n, h):
-            of = staged_share(n, h)
+        def unstage(copy, n, g):
+            of = staged_share(n, g)
             copy(
-                out=grouped_of[(n, h)][:, of, :].rearrange("p c j -> p (c j)"),
-                in_=staged_of[(n, h)][:, 0 : PACK * (of.stop - of.start)],
+                out=grouped_of[(n, g)][:, of, :].rearrange("p c j -> p (c j)"),
+                in_=staged_of[(n, g)][:, 0 : PACK * (of.stop - of.start)],
             )
 
-        def regroup_on_scalar(n, h):
-            share = slice(0, scalar_columns(n, h))
+        def regroup_on_scalar(n, g):
+            share = slice(0, scalar_columns(n, g))
             nc.scalar.copy(
-                out=grouped_of[(n, h)][:, share, :].rearrange("p (c r) j -> p c j r", r=RUN),
-                in_=raw_of[(n, h)][:, :, share].rearrange("p j (c r) -> p c j r", r=RUN),
+                out=grouped_of[(n, g)][:, share, :].rearrange("p (c r) j -> p c j r", r=RUN),
+                in_=raw_of[(n, g)][:, :, share].rearrange("p j (c r) -> p c j r", r=RUN),
             )
 
-        def quantise(n, h):
-            codes = code_pool.tile([P, STREAMS, HALF], U32, align_bytes=64)
-            planes = code_pool.tile([P, STREAMS, HALF], U8, align_bytes=64)
+        def quantise(n, g):
+            codes = code_pool.tile([P, COLUMNS], U32, align_bytes=64)
+            planes = code_pool.tile([P, COLUMNS], U8, align_bytes=64)
             nc.vector.quantize_mx(
-                out=codes[:].rearrange("p g w -> p (g w)").bitcast(FP8X4),
-                scales=planes[:].rearrange("p g w -> p (g w)"),
-                in_=grouped_of[(n, h)][:].rearrange("p c j -> p (c j)"),
+                out=codes[:].bitcast(FP8X4),
+                scales=planes[:],
+                in_=grouped_of[(n, g)][:].rearrange("p c j -> p (c j)"),
             )
-            codes_of[(n, h)] = codes
-            planes_of[(n, h)] = planes
+            codes_of[(n, g)] = codes
+            planes_of[(n, g)] = planes
 
-        def project(n, h, i):
-            if h == 0:
+        def project(n, i, h, g):
+            if h == 0 and g == 0:
                 y = psum.tile([P, HALVES, HALF], F32)
                 y_of[(n, i)] = y
-            for g in range(STREAMS):
-                nc.tensor.matmul_mx(
-                    out=y_of[(n, i)][:, h, :],
-                    lhsT=w_codes[:, i, g, :].bitcast(FP8X4),
-                    lhsT_scale=w_planes[:, i, g, :],
-                    rhs=codes_of[(n, h)][:, g, :].bitcast(FP8X4),
-                    rhs_scale=planes_of[(n, h)][:, g, :],
-                    start=(g == 0),
-                    stop=(g == STREAMS - 1),
-                )
+            half = slice(h * HALF, (h + 1) * HALF)
+            nc.tensor.matmul_mx(
+                out=y_of[(n, i)][:, h, :],
+                lhsT=w_codes[:, i, g, :].bitcast(FP8X4),
+                lhsT_scale=w_planes[:, i, g, :],
+                rhs=codes_of[(n, g)][:, half].bitcast(FP8X4),
+                rhs_scale=planes_of[(n, g)][:, half],
+                start=(g == 0),
+                stop=(g == STREAMS - 1),
+            )
 
         def first_exp(n, i):
             a = soft_pool.tile([P, HALVES, HALF], F32)
@@ -256,19 +256,20 @@ def tile_fr_pa_t_kernel(
                     accum_out=value_sum[:, h, BATCH * i + n : BATCH * i + n + 1],
                 )
 
-        units = BATCH * HALVES
+        units = BATCH * STREAMS
 
         def unit(u):
-            return divmod(u, HALVES)
+            return divmod(u, STREAMS)
 
         for p in range(-3, units + 2):
             for u in (p + 2, p + 3):
                 if 0 <= u < units and (u == p + 3) == (u >= FIRST_VECTOR_UNSTAGE):
                     stage_on_tensor(*unit(u))
             if 0 <= p < units:
-                n, h = unit(p)
-                quantise(n, h)
-                project(n, h, 0)
+                n, g = unit(p)
+                quantise(n, g)
+                for h in range(HALVES):
+                    project(n, 0, h, g)
             if 0 <= p + 1 < VECTOR_UNITS:
                 regroup_on_vector(*unit(p + 1))
             if 0 <= p + 3 < units:
@@ -284,9 +285,10 @@ def tile_fr_pa_t_kernel(
                         first_exp(back, i)
             if 0 <= back < BATCH and second:
                 weigh(back, 0)
-            if 0 <= p < units and p % HALVES == HALVES - 1:
+            if 0 <= p < units and g == STREAMS - 1:
                 for h in range(HALVES):
-                    project(p // HALVES, h, 1)
+                    for k in range(STREAMS):
+                        project(n, 1, h, k)
             if 0 <= back < BATCH and second:
                 weigh(back, 1, gated=unit(p + 3) if p + 3 < units else None)
             if 0 <= back < BATCH and not second:

@@ -26,12 +26,13 @@ OUT = 128
 RUN = 4
 COLUMNS = POSITIONS
 PRODUCT_COLUMNS = 2 * HALF // PACK
-STAGED_COLUMNS = 204
-SCALAR_COLUMNS = 324
-EARLY_SCALAR_COLUMNS = 188
+STAGED_COLUMNS = 200
+SCALAR_COLUMNS = 328
+EARLY_SCALAR_COLUMNS = 192
 VECTOR_UNITS = 4
 FIRST_VECTOR_UNSTAGE = 5
-OVERLAP = 1
+OVERLAP = 8
+LINE = 8
 MATMUL_COLUMNS = 128
 
 FLOPS = 2 * BATCH * HEADS * OUT * STREAMS * P * PACK * POSITIONS
@@ -165,9 +166,9 @@ def tile_fr_pa_t_kernel(
                 share = slice(first, min(first + MATMUL_COLUMNS, of.stop))
                 into = slice(PACK * (share.start - of.start), PACK * (share.stop - of.start))
                 nc.tensor.matmul(
-                    out=staged[:, into].rearrange("p (c j) -> p c j", j=PACK),
+                    out=staged[:, into].rearrange("p (c r j) -> p c j r", r=LINE, j=PACK),
                     lhsT=identity_bf16[:],
-                    rhs=raw_of[(n, g)][:, :, share].rearrange("p j c -> p c j"),
+                    rhs=raw_of[(n, g)][:, :, share].rearrange("p j (c r) -> p c j r", r=LINE),
                     start=True,
                     stop=True,
                 )

@@ -32,7 +32,6 @@ EARLY_SCALAR_COLUMNS = 192
 VECTOR_UNITS = 4
 FIRST_VECTOR_UNSTAGE = 5
 OVERLAP = 8
-LINE = 8
 MATMUL_COLUMNS = 128
 
 FLOPS = 2 * BATCH * HEADS * OUT * STREAMS * P * PACK * POSITIONS
@@ -151,8 +150,8 @@ def tile_fr_pa_t_kernel(
         def regroup_on_gpsimd(n, g):
             share = helper_share(n, g)
             nc.gpsimd.tensor_scalar(
-                out=grouped_of[(n, g)][:, share, :],
-                in0=raw_of[(n, g)][:, :, share].rearrange("p j c -> p c j"),
+                out=grouped_of[(n, g)][:, share, :].rearrange("p (c r) j -> p c j r", r=RUN),
+                in0=raw_of[(n, g)][:, :, share].rearrange("p j (c r) -> p c j r", r=RUN),
                 scalar1=1.0,
                 scalar2=0.0,
                 op0=ALU.mult,
@@ -166,9 +165,9 @@ def tile_fr_pa_t_kernel(
                 share = slice(first, min(first + MATMUL_COLUMNS, of.stop))
                 into = slice(PACK * (share.start - of.start), PACK * (share.stop - of.start))
                 nc.tensor.matmul(
-                    out=staged[:, into].rearrange("p (c r j) -> p c j r", r=LINE, j=PACK),
+                    out=staged[:, into].rearrange("p (c j) -> p j c", j=PACK),
                     lhsT=identity_bf16[:],
-                    rhs=raw_of[(n, g)][:, :, share].rearrange("p j (c r) -> p c j r", r=LINE),
+                    rhs=raw_of[(n, g)][:, :, share],
                     start=True,
                     stop=True,
                 )

@@ -26,12 +26,11 @@ OUT = 128
 RUN = 4
 COLUMNS = POSITIONS
 PRODUCT_COLUMNS = 2 * HALF // PACK
-STAGED_COLUMNS = 200
-SCALAR_COLUMNS = 328
-EARLY_SCALAR_COLUMNS = 192
+STAGED_COLUMNS = 204
+SCALAR_COLUMNS = 244
+EARLY_SCALAR_COLUMNS = 188
 VECTOR_UNITS = 4
-FIRST_VECTOR_UNSTAGE = 5
-OVERLAP = 8
+FIRST_GATED = VECTOR_UNITS + 1
 MATMUL_COLUMNS = 128
 
 FLOPS = 2 * BATCH * HEADS * OUT * STREAMS * P * PACK * POSITIONS
@@ -130,15 +129,12 @@ def tile_fr_pa_t_kernel(
         def scalar_columns(n, g):
             return EARLY_SCALAR_COLUMNS if STREAMS * n + g < VECTOR_UNITS else SCALAR_COLUMNS
 
-        def vector_unstages(n, g):
-            return STREAMS * n + g >= FIRST_VECTOR_UNSTAGE and g == 1
-
         def helper_share(n, g):
             return slice(scalar_columns(n, g) + STAGED_COLUMNS, COLUMNS)
 
         def staged_share(n, g):
             first = scalar_columns(n, g)
-            return slice(first, first + STAGED_COLUMNS + (OVERLAP if vector_unstages(n, g) else 0))
+            return slice(first, first + STAGED_COLUMNS)
 
         def regroup_on_vector(n, g):
             share = helper_share(n, g)
@@ -158,6 +154,9 @@ def tile_fr_pa_t_kernel(
                 op1=ALU.add,
             )
 
+        def gate_gpsimd(n, g):
+            nc.vector.memset(grouped_of[(n, g)][:, COLUMNS - 1, 0:1], 1.0)
+
         def stage_on_tensor(n, g):
             staged = stage_pool.tile([P, 2 * HALF], BF16)
             of = staged_share(n, g)
@@ -173,9 +172,9 @@ def tile_fr_pa_t_kernel(
                 )
             staged_of[(n, g)] = staged
 
-        def unstage(copy, n, g):
+        def unstage_on_scalar(n, g):
             of = staged_share(n, g)
-            copy(
+            nc.scalar.copy(
                 out=grouped_of[(n, g)][:, of, :].rearrange("p c j -> p (c j)"),
                 in_=staged_of[(n, g)][:, 0 : PACK * (of.stop - of.start)],
             )
@@ -262,9 +261,8 @@ def tile_fr_pa_t_kernel(
             return divmod(u, STREAMS)
 
         for p in range(-3, units + 2):
-            for u in (p + 2, p + 3):
-                if 0 <= u < units and (u == p + 3) == (u >= FIRST_VECTOR_UNSTAGE):
-                    stage_on_tensor(*unit(u))
+            if 0 <= p + 2 < units:
+                stage_on_tensor(*unit(p + 2))
             if 0 <= p < units:
                 n, g = unit(p)
                 quantise(n, g)
@@ -274,8 +272,6 @@ def tile_fr_pa_t_kernel(
                 regroup_on_vector(*unit(p + 1))
             if 0 <= p + 3 < units:
                 new_grouped(*unit(p + 3))
-            if VECTOR_UNITS <= p + 3 < FIRST_VECTOR_UNSTAGE:
-                regroup_on_gpsimd(*unit(p + 3))
             back, second = divmod(p - 2, 2)
             if 0 <= back < BATCH:
                 for i in range(HEADS):
@@ -294,14 +290,13 @@ def tile_fr_pa_t_kernel(
             if 0 <= back < BATCH and not second:
                 for i in range(HEADS):
                     top(back, i)
-            if 0 <= p + 3 < units and vector_unstages(*unit(p + 3)):
-                unstage(nc.vector.tensor_copy, *unit(p + 3))
-            if FIRST_VECTOR_UNSTAGE <= p + 3 < units:
+            if VECTOR_UNITS <= p + 3 < units:
+                if p + 3 >= FIRST_GATED and not second:
+                    gate_gpsimd(*unit(p + 3))
                 regroup_on_gpsimd(*unit(p + 3))
             if 0 <= p + 2 < units:
                 regroup_on_scalar(*unit(p + 2))
-                if not vector_unstages(*unit(p + 2)):
-                    unstage(nc.scalar.copy, *unit(p + 2))
+                unstage_on_scalar(*unit(p + 2))
 
         for i in range(HEADS):
             of_head = slice(BATCH * i, BATCH * (i + 1))

@@ -27,7 +27,7 @@ RUN = 4
 COLUMNS = POSITIONS
 PRODUCT_COLUMNS = 2 * HALF // PACK
 STAGED_COLUMNS = 204
-SCALAR_COLUMNS = 244
+SCALAR_COLUMNS = 240
 EARLY_SCALAR_COLUMNS = 188
 VECTOR_UNITS = 4
 FIRST_GATED = VECTOR_UNITS + 1
@@ -98,7 +98,7 @@ def tile_fr_pa_t_kernel(
                 load_x(n, g, slice(k * COLUMNS // pieces, (k + 1) * COLUMNS // pieces))
             if u == 0:
                 load_weight(0)
-            if u == 1:
+            if u == 2:
                 load_weight(1)
         identity_bf16 = keep.tile([P, P], BF16)
         make_identity(nc, identity_bf16[:])
@@ -215,7 +215,7 @@ def tile_fr_pa_t_kernel(
         def first_exp(n, i):
             a = soft_pool.tile([P, HALVES, HALF], F32)
             for h in range(HALVES):
-                nc.scalar.activation(out=a[:, h, :], in_=y_of[(n, i)][:, h, :], func=EXP, bias=bias_of[i][:])
+                nc.scalar.activation(out=a[:, h, :], in_=y_of[(n, i)][:, h, :], func=EXP, bias=bias_f32[:, i : i + 1])
             a_of[(n, i)] = a
 
         def top(n, i):
@@ -261,7 +261,7 @@ def tile_fr_pa_t_kernel(
             return divmod(u, STREAMS)
 
         for p in range(-3, units + 2):
-            if 0 <= p + 2 < units:
+            if 0 <= p + 2 < units and p != STREAMS - 1:
                 stage_on_tensor(*unit(p + 2))
             if 0 <= p < units:
                 n, g = unit(p)
@@ -277,7 +277,7 @@ def tile_fr_pa_t_kernel(
                 for i in range(HEADS):
                     if second:
                         second_exp(back, i)
-                    else:
+                    elif back > 0:
                         first_exp(back, i)
             if 0 <= back < BATCH and second:
                 weigh(back, 0)
@@ -285,6 +285,8 @@ def tile_fr_pa_t_kernel(
                 for h in range(HALVES):
                     for k in range(STREAMS):
                         project(n, 1, h, k)
+            if p == STREAMS - 1:
+                stage_on_tensor(*unit(p + 2))
             if 0 <= back < BATCH and second:
                 weigh(back, 1, gated=unit(p + 3) if p + 3 < units else None)
             if 0 <= back < BATCH and not second:
@@ -294,6 +296,9 @@ def tile_fr_pa_t_kernel(
                 if p + 3 >= FIRST_GATED and not second:
                     gate_gpsimd(*unit(p + 3))
                 regroup_on_gpsimd(*unit(p + 3))
+            if p == STREAMS - 1:
+                for i in range(HEADS):
+                    first_exp(0, i)
             if 0 <= p + 2 < units:
                 regroup_on_scalar(*unit(p + 2))
                 unstage_on_scalar(*unit(p + 2))

from contextlib import ExitStack

import concourse.mybir as mybir
from concourse.masks import make_identity

FP8X4 = mybir.dt.float8_e4m3fn_x4
BF16 = mybir.dt.bfloat16
F32 = mybir.dt.float32
U32 = mybir.dt.uint32
U8 = mybir.dt.uint8
I32 = mybir.dt.int32
EXP = mybir.ActivationFunctionType.Exp
COPY = mybir.ActivationFunctionType.Copy
ALU = mybir.AluOpType
AXIS_X = mybir.AxisListType.X

P = 128
PACK = 4
BATCH = 8
STREAMS = 2
POSITIONS = 1024
HALF = 512
HALVES = POSITIONS // HALF
HEADS = 2
OUT = 128
RUN = 4
COLUMNS = POSITIONS
PRODUCT_COLUMNS = 2 * HALF // PACK
STAGED_COLUMNS = 204
SCALAR_COLUMNS = 240
EARLY_SCALAR_COLUMNS = 188
VECTOR_UNITS = 4
FIRST_GATED = VECTOR_UNITS + 1
MATMUL_COLUMNS = 128

FLOPS = 2 * BATCH * HEADS * OUT * STREAMS * P * PACK * POSITIONS


def tile_fr_pa_t_kernel(
    tc, x1, x2, c1_w_words, c1_w_scales, c1_b, c2_w_words, c2_w_scales, c2_b, out_0, out_1
):
    nc = tc.nc
    streams = (x1, x2)
    weights = ((c1_w_words, c1_w_scales, c1_b), (c2_w_words, c2_w_scales, c2_b))

    with ExitStack() as ctx:
        keep = ctx.enter_context(tc.tile_pool(name="keep", bufs=1))
        group_pool = ctx.enter_context(tc.tile_pool(name="group", bufs=3))
        code_pool = ctx.enter_context(tc.tile_pool(name="code", bufs=4))
        soft_pool = ctx.enter_context(tc.tile_pool(name="soft", bufs=3))
        psum = ctx.enter_context(tc.psum_pool(name="psum", bufs=3))
        stage_pool = ctx.enter_context(tc.psum_pool(name="stage", bufs=2))
        ctx.enter_context(tc.manual_schedule())

        raw_of = {}
        grouped_of = {}
        staged_of = {}
        codes_of = {}
        planes_of = {}
        y_of = {}
        a_of = {}
        e_of = {}

        w_codes = keep.tile([P, HEADS, STREAMS, OUT], U32, align_bytes=64)
        w_planes = keep.tile([P, HEADS, STREAMS, OUT], U8, align_bytes=64)
        nc.vector.memset(w_planes[:].rearrange("p i g o -> p (i g o)").bitcast(I32), 0)
        bias_of = {}

        def load_weight(i):
            words, scales, b = weights[i]
            for quadrant in range(4):
                nc.sync.dma_start(
                    out=w_planes[32 * quadrant : 32 * quadrant + 4, i].bitcast(I32),
                    in_=scales[:, 4 * quadrant : 4 * quadrant + 4, :].rearrange("g r o -> r g o").bitcast(I32),
                )
            nc.sync.dma_start(
                out=w_codes[:, i].bitcast(I32),
                in_=words.rearrange("g p o t -> p g (o t)").bitcast(I32),
            )

        def load_bias(i):
            words, scales, b = weights[i]
            bias = keep.tile([P, 1], BF16, name="bias_%d" % i)
            nc.gpsimd.dma_start(out=bias[:], in_=b.rearrange("(o one) -> o one", one=1))
            bias_of[i] = bias

        def load_x(n, g, columns):
            if columns.start == 0:
                raw = keep.tile([P, PACK, COLUMNS], BF16, name="raw_%d_%d" % (n, g))
                raw_of[(n, g)] = raw
            rows = streams[g][n].rearrange("(p j) a b -> p j (a b)", j=PACK)
            nc.sync.dma_start(out=raw_of[(n, g)][:, :, columns], in_=rows[:, :, columns])

        for u in range(BATCH * STREAMS):
            n, g = divmod(u, STREAMS)
            pieces = HALVES if u == 0 else 1
            for k in range(pieces):
                load_x(n, g, slice(k * COLUMNS // pieces, (k + 1) * COLUMNS // pieces))
            if u == 0:
                load_weight(0)
            if u == 2:
                load_weight(1)
        identity_bf16 = keep.tile([P, P], BF16)
        make_identity(nc, identity_bf16[:])
        load_bias(0)
        load_bias(1)

        warm = keep.tile([P, 1], F32)
        nc.vector.memset(warm[:], 0.0)
        nc.scalar.activation(out=warm[:], in_=warm[:], func=EXP)

        identity = keep.tile([P, P], F32)
        make_identity(nc, identity[:])
        neg_top = keep.tile([P, HEADS, BATCH], F32)
        weight_sum = keep.tile([P, P], F32)
        nc.gpsimd.memset(weight_sum[:], 1.0)
        value_sum = keep.tile([P, HALVES, P], F32)
        nc.gpsimd.memset(value_sum[:].rearrange("p h c -> p (h c)"), 0.0)
        bias_sum = keep.tile([P, P], F32)
        nc.gpsimd.memset(bias_sum[:], 0.0)
        bias_f32 = keep.tile([P, HEADS], F32)
        for i in range(HEADS):
            nc.gpsimd.tensor_copy(out=bias_f32[:, i : i + 1], in_=bias_of[i][:])

        def new_grouped(n, g):
            grouped = group_pool.tile([P, COLUMNS, PACK], BF16, align_bytes=64)
            grouped_of[(n, g)] = grouped

        def scalar_columns(n, g):
            return EARLY_SCALAR_COLUMNS if STREAMS * n + g < VECTOR_UNITS else SCALAR_COLUMNS

        def helper_share(n, g):
            return slice(scalar_columns(n, g) + STAGED_COLUMNS, COLUMNS)

        def staged_share(n, g):
            first = scalar_columns(n, g)
            return slice(first, first + STAGED_COLUMNS)

        def regroup_on_vector(n, g):
            share = helper_share(n, g)
            nc.vector.tensor_copy(
                out=grouped_of[(n, g)][:, share, :].rearrange("p (c r) j -> p c j r", r=RUN),
                in_=raw_of[(n, g)][:, :, share].rearrange("p j (c r) -> p c j r", r=RUN),
            )

        def regroup_on_gpsimd(n, g):
            share = helper_share(n, g)
            nc.gpsimd.tensor_scalar(
                out=grouped_of[(n, g)][:, share, :].rearrange("p (c r) j -> p c j r", r=RUN),
                in0=raw_of[(n, g)][:, :, share].rearrange("p j (c r) -> p c j r", r=RUN),
                scalar1=1.0,
                scalar2=0.0,
                op0=ALU.mult,
                op1=ALU.add,
            )

        def gate_gpsimd(n, g):
            nc.vector.memset(grouped_of[(n, g)][:, COLUMNS - 1, 0:1], 1.0)

        def stage_on_tensor(n, g):
            staged = stage_pool.tile([P, 2 * HALF], BF16)
            of = staged_share(n, g)
            for first in range(of.start, of.stop, MATMUL_COLUMNS):
                share = slice(first, min(first + MATMUL_COLUMNS, of.stop))
                into = slice(PACK * (share.start - of.start), PACK * (share.stop - of.start))
                nc.tensor.matmul(
                    out=staged[:, into].rearrange("p (c j) -> p j c", j=PACK),
                    lhsT=identity_bf16[:],
                    rhs=raw_of[(n, g)][:, :, share],
                    start=True,
                    stop=True,
                )
            staged_of[(n, g)] = staged

        def unstage_on_scalar(n, g):
            of = staged_share(n, g)
            nc.scalar.copy(
                out=grouped_of[(n, g)][:, of, :].rearrange("p c j -> p (c j)"),
                in_=staged_of[(n, g)][:, 0 : PACK * (of.stop - of.start)],
            )

        def regroup_on_scalar(n, g):
            share = slice(0, scalar_columns(n, g))
            nc.scalar.copy(
                out=grouped_of[(n, g)][:, share, :].rearrange("p (c r) j -> p c j r", r=RUN),
                in_=raw_of[(n, g)][:, :, share].rearrange("p j (c r) -> p c j r", r=RUN),
            )

        def quantise(n, g):
            codes = code_pool.tile([P, COLUMNS], U32, align_bytes=64)
            planes = code_pool.tile([P, COLUMNS], U8, align_bytes=64)
            nc.vector.quantize_mx(
                out=codes[:].bitcast(FP8X4),
                scales=planes[:],
                in_=grouped_of[(n, g)][:].rearrange("p c j -> p (c j)"),
            )
            codes_of[(n, g)] = codes
            planes_of[(n, g)] = planes

        def project(n, i, h, g):
            if h == 0 and g == 0:
                y = psum.tile([P, HALVES, HALF], F32)
                y_of[(n, i)] = y
            half = slice(h * HALF, (h + 1) * HALF)
            nc.tensor.matmul_mx(
                out=y_of[(n, i)][:, h, :],
                lhsT=w_codes[:, i, g, :].bitcast(FP8X4),
                lhsT_scale=w_planes[:, i, g, :],
                rhs=codes_of[(n, g)][:, half].bitcast(FP8X4),
                rhs_scale=planes_of[(n, g)][:, half],
                start=(g == 0),
                stop=(g == STREAMS - 1),
            )

        def first_exp(n, i):
            a = soft_pool.tile([P, HALVES, HALF], F32)
            for h in range(HALVES):
                nc.scalar.activation(out=a[:, h, :], in_=y_of[(n, i)][:, h, :], func=EXP, bias=bias_f32[:, i : i + 1])
            a_of[(n, i)] = a

        def top(n, i):
            nc.vector.tensor_reduce(
                out=neg_top[:, i, n : n + 1],
                in_=a_of[(n, i)][:].rearrange("p h w -> p (h w)"),
                axis=AXIS_X,
                op=ALU.max,
                negate=True,
            )

        def second_exp(n, i):
            e = soft_pool.tile([P, HALVES, HALF], F32)
            nc.scalar.activation(
                out=e[:].rearrange("p h w -> p (h w)"),
                in_=a_of[(n, i)][:].rearrange("p h w -> p (h w)"),
                func=EXP,
                bias=neg_top[:, i, n : n + 1],
                accum_out=weight_sum[:, BATCH * i + n : BATCH * i + n + 1],
            )
            e_of[(n, i)] = e

        def weigh(n, i, gated=None):
            e = e_of[(n, i)]
            for h in range(HALVES):
                products = e[:, h, :]
                if h == HALVES - 1 and gated is not None:
                    place = grouped_of[gated][:, COLUMNS - PRODUCT_COLUMNS : COLUMNS, :]
                    products = place.rearrange("p c j -> p (c j)").bitcast(F32)
                nc.vector.scalar_tensor_tensor(
                    out=products,
                    in0=e[:, h, :],
                    scalar=1.0,
                    in1=y_of[(n, i)][:, h, :],
                    op0=ALU.mult,
                    op1=ALU.mult,
                    accum_out=value_sum[:, h, BATCH * i + n : BATCH * i + n + 1],
                )

        units = BATCH * STREAMS

        def unit(u):
            return divmod(u, STREAMS)

        for p in range(-3, units + 2):
            if 0 <= p + 2 < units and p != STREAMS - 1:
                stage_on_tensor(*unit(p + 2))
            if 0 <= p < units:
                n, g = unit(p)
                quantise(n, g)
                for h in range(HALVES):
                    project(n, 0, h, g)
            if 0 <= p + 1 < VECTOR_UNITS:
                regroup_on_vector(*unit(p + 1))
            if 0 <= p + 3 < units:
                new_grouped(*unit(p + 3))
            back, second = divmod(p - 2, 2)
            if 0 <= back < BATCH:
                for i in range(HEADS):
                    if second:
                        second_exp(back, i)
                    elif back > 0:
                        first_exp(back, i)
            if 0 <= back < BATCH and second:
                weigh(back, 0)
            if 0 <= p < units and g == STREAMS - 1:
                for h in range(HALVES):
                    for k in range(STREAMS):
                        project(n, 1, h, k)
            if p == STREAMS - 1:
                stage_on_tensor(*unit(p + 2))
            if 0 <= back < BATCH and second:
                weigh(back, 1, gated=unit(p + 3) if p + 3 < units else None)
            if 0 <= back < BATCH and not second:
                for i in range(HEADS):
                    top(back, i)
            if VECTOR_UNITS <= p + 3 < units:
                if p + 3 >= FIRST_GATED and not second:
                    gate_gpsimd(*unit(p + 3))
                regroup_on_gpsimd(*unit(p + 3))
            if p == STREAMS - 1:
                for i in range(HEADS):
                    first_exp(0, i)
            if 0 <= p + 2 < units:
                regroup_on_scalar(*unit(p + 2))
                unstage_on_scalar(*unit(p + 2))

        for i in range(HEADS):
            of_head = slice(BATCH * i, BATCH * (i + 1))
            nc.scalar.activation(
                out=bias_sum[:, of_head], in_=weight_sum[:, of_head], func=COPY, scale=bias_f32[:, i : i + 1]
            )
        flipped_weight = psum.tile([P, HALVES, HALF], F32, tag="y")
        nc.tensor.transpose(flipped_weight[:, 0, 0:P], weight_sum[:], identity[:])
        inverse = keep.tile([P, P], F32)
        nc.vector.reciprocal(out=inverse[:], in_=flipped_weight[:, 0, 0:P])
        flipped = psum.tile([P, HALVES, HALF], F32, tag="y")
        terms = [bias_sum[:]] + [value_sum[:, h, :] for h in range(HALVES)]
        for k, term in enumerate(terms):
            nc.tensor.matmul(
                out=flipped[:, 0, 0:P],
                lhsT=term,
                rhs=identity[:],
                is_transpose=True,
                start=(k == 0),
                stop=(k == len(terms) - 1),
            )
        rows_out = keep.tile([P, P], F32)
        nc.vector.tensor_tensor(out=rows_out[:], in0=flipped[:, 0, 0:P], in1=inverse[:], op=ALU.mult)
        nc.sync.dma_start(out=out_0, in_=rows_out[0:BATCH, :])
        nc.scalar.dma_start(out=out_1, in_=rows_out[BATCH : 2 * BATCH, :])
